import numpy as np
import ml_dtypes

BF16 = ml_dtypes.bfloat16


def bf(x):
    return np.asarray(x, np.float32).astype(BF16)


def f32(x):
    return np.asarray(x, np.float32)


def f64(x):
    return np.asarray(x).astype(np.float64)


def striped(idx):
    return np.tile(idx.reshape(-1, 16).T, (8, 1))


C, S, N, B, T, NH, HD, HALF = 512, 4096, 2048, 4, 512, 4, 128, 256
EPS = 1e-6
PE_BASE = 10000.0


def pos_table():
    place = np.arange(T, dtype=np.float32)[:, None]
    div = np.exp(np.arange(HALF, dtype=np.float32) * np.float32(-np.log(PE_BASE) / (HALF - 1)))
    ang = place * div
    return np.tile(np.concatenate([np.sin(ang), np.cos(ang)], axis=-1).T, (1, B))


def heads(a):
    return a.reshape(NH, HD, B, T).transpose(0, 2, 3, 1)


def setup_inputs():
    return {
        "emb": f32(np.random.standard_normal((C, S))),
        "pos": f32(pos_table()),
        "ln_w": f32(1.0 + 0.1 * np.random.standard_normal((C, 1))),
        "ln_b": f32(0.1 * np.random.standard_normal((C, 1))),
        "wq": bf(np.random.standard_normal((C, C)) * np.sqrt(2.0 / C)),
        "wk": bf(np.random.standard_normal((C, C)) * np.sqrt(2.0 / C)),
        "wv": bf(np.random.standard_normal((C, C)) / np.sqrt(C)),
        "wp": bf(np.random.standard_normal((C, C)) * 2.0 / np.sqrt(C)),
        "offs": striped(np.random.permutation(np.tile(np.arange(S), 2))[:N]),
    }


def reference(emb, pos, ln_w, ln_b, wq, wk, wv, wp, offs):
    idx = offs[:16].T.reshape(-1)
    x = f64(emb)[:, idx] + f64(pos)
    mu = x.mean(axis=0, keepdims=True)
    var = ((x - mu) ** 2).mean(axis=0, keepdims=True)
    h = (x - mu) / np.sqrt(var + EPS) * f64(ln_w) + f64(ln_b)
    q = heads(f64(wq).T @ h)
    k = heads(f64(wk).T @ h)
    v = heads(f64(wv).T @ h)
    sc = (q @ k.transpose(0, 1, 3, 2)) / np.sqrt(HD)
    e = np.exp(sc - sc.max(axis=-1, keepdims=True))
    att = e / e.sum(axis=-1, keepdims=True)
    y = (att @ v).transpose(0, 3, 1, 2).reshape(C, N)
    return x + f64(wp).T @ y

@@ -1,0 +1,185 @@
+import concourse.mybir as mybir
+
+F32 = mybir.dt.float32
+BF16 = mybir.dt.bfloat16
+U16 = mybir.dt.uint16
+ALU = mybir.AluOpType
+FUNC = mybir.ActivationFunctionType
+
+P = 128
+C = 512
+CB = C // P
+S = 4096
+B = 4
+T = 512
+TB = T // P
+N = B * T
+EPS = 1e-6
+SCORE_SCALE = P**-0.5
+
+FLOPS = 2 * (4 * C * C * N + 2 * B * CB * T * T * P)
+
+
+def tile_transformernet_b_kernel(tc, emb, pos, ln_w, ln_b, wq, wk, wv, wp, offs, out):
+    nc = tc.nc
+    with (
+        tc.tile_pool(name="held", bufs=1) as held,
+        tc.psum_pool(name="psum_mm", bufs=2) as psum_mm,
+    ):
+        offsets = held.tile([P, N // 16], U16, name="offsets")
+        nc.sync.dma_start(offsets[:], offs)
+
+        gain = held.tile([P, CB], F32, name="gain")
+        shift = held.tile([P, CB], F32, name="shift")
+        with nc.allow_non_contiguous_dma(reason="one value to a partition, 4 to a row"):
+            nc.scalar.dma_start(gain[:], ln_w.rearrange("(a p) o -> p (a o)", p=P))
+            nc.scalar.dma_start(shift[:], ln_b.rearrange("(a p) o -> p (a o)", p=P))
+
+        mean_w = held.tile([P, P], BF16, name="mean_w")
+        nc.vector.memset(mean_w[:], 1.0 / C)
+        ones = held.tile([P, P], BF16, name="ones")
+        nc.vector.memset(ones[:], 1.0)
+        eps = held.tile([P, 1], F32, name="eps")
+        nc.vector.memset(eps[:], EPS)
+
+        wq_sb = held.tile([P, CB, C], BF16, name="wq_sb")
+        wk_sb = held.tile([P, CB, C], BF16, name="wk_sb")
+        wv_sb = held.tile([P, CB, C], BF16, name="wv_sb")
+        wp_sb = held.tile([P, CB, C], BF16, name="wp_sb")
+
+        x = [held.tile([P, N], F32, name="x%d" % cb) for cb in range(CB)]
+        h = [held.tile([P, CB, T], BF16, name="h%d" % b) for b in range(B)]
+
+        with (
+            tc.tile_pool(name="lookup", bufs=1) as lookup,
+            tc.tile_pool(name="norm", bufs=2) as norm,
+            tc.psum_pool(name="psum_stat", bufs=2) as psum_stat,
+        ):
+            table = []
+            place = []
+            for cb in range(CB):
+                rows = slice(cb * P, (cb + 1) * P)
+                place.append(lookup.tile([P, T], F32, name="place%d" % cb))
+                nc.sync.dma_start(place[cb][:], pos[rows, 0:T])
+                table.append(lookup.tile([P, S], F32, name="table%d" % cb))
+                nc.sync.dma_start(table[cb][:], emb[rows, :])
+            for w_sb, w in ((wq_sb, wq), (wk_sb, wk), (wv_sb, wv), (wp_sb, wp)):
+                nc.sync.dma_start(w_sb[:], w.rearrange("(a p) o -> p a o", p=P))
+
+            for b in range(B):
+                cols = slice(b * T, (b + 1) * T)
+                piece = offsets[:, b * T // 16 : (b + 1) * T // 16]
+
+                for cb in range(CB):
+                    nc.vector.tensor_tensor(
+                        x[cb][:, cols], table[cb][:].indirect(piece), place[cb][:], ALU.add
+                    )
+
+                x_bf = norm.tile([P, CB, T], BF16, name="x_bf")
+                mean_ps = psum_stat.tile([P, T], F32, name="mean_ps", tag="stat")
+                for cb in range(CB):
+                    nc.gpsimd.tensor_scalar(x_bf[:, cb, :], x[cb][:, cols], 1.0, None, ALU.mult)
+                    nc.tensor.matmul(
+                        mean_ps[:], mean_w[:], x_bf[:, cb, :], start=cb == 0, stop=cb == CB - 1
+                    )
+
+                centred = norm.tile([P, CB, T], F32, name="centred")
+                squared = norm.tile([P, CB, T], BF16, name="squared")
+                var_ps = psum_stat.tile([P, T], F32, name="var_ps", tag="stat")
+                for cb in range(CB):
+                    nc.vector.tensor_tensor(centred[:, cb, :], x[cb][:, cols], mean_ps[:], ALU.subtract)
+                    nc.scalar.activation(squared[:, cb, :], centred[:, cb, :], FUNC.Square)
+                    nc.tensor.matmul(
+                        var_ps[:], mean_w[:], squared[:, cb, :], start=cb == 0, stop=cb == CB - 1
+                    )
+                rstd = norm.tile([P, T], F32, name="rstd")
+                nc.scalar.activation(rstd[:], var_ps[:], FUNC.Abs_reciprocal_sqrt, bias=eps[:])
+
+                for cb in range(CB):
+                    nc.gpsimd.tensor_tensor(centred[:, cb, :], centred[:, cb, :], rstd[:], ALU.mult)
+                    nc.gpsimd.tensor_scalar(
+                        h[b][:, cb, :],
+                        centred[:, cb, :],
+                        gain[:, cb : cb + 1],
+                        shift[:, cb : cb + 1],
+                        ALU.mult,
+                        ALU.add,
+                    )
+
+        with (
+            tc.tile_pool(name="qkv", bufs=2) as qkv,
+            tc.tile_pool(name="attn", bufs=2) as attn,
+            tc.psum_pool(name="psum_y", bufs=1) as psum_y,
+            tc.psum_pool(name="psum_sc", bufs=4) as psum_sc,
+        ):
+            for b in range(B):
+                cols = slice(b * T, (b + 1) * T)
+
+                q = qkv.tile([P, CB, T], BF16, name="q")
+                k = qkv.tile([P, CB, T], BF16, name="k")
+                for w_sb, dest in ((wq_sb, q), (wk_sb, k)):
+                    for ob in range(CB):
+                        mm_ps = psum_mm.tile([P, T], F32, name="mm_ps")
+                        for cb in range(CB):
+                            nc.tensor.matmul(
+                                mm_ps[:],
+                                w_sb[:, cb, ob * P : (ob + 1) * P],
+                                h[b][:, cb, :],
+                                start=cb == 0,
+                                stop=cb == CB - 1,
+                            )
+                        nc.scalar.copy(dest[:, ob, :], mm_ps[:])
+
+                v_t = qkv.tile([P, TB, C], BF16, name="v_t")
+                for ub in range(TB):
+                    mm_ps = psum_mm.tile([P, T], F32, name="mm_ps")
+                    for cb in range(CB):
+                        nc.tensor.matmul(
+                            mm_ps[:],
+                            h[b][:, cb, ub * P : (ub + 1) * P],
+                            wv_sb[:, cb, :],
+                            start=cb == 0,
+                            stop=cb == CB - 1,
+                        )
+                    nc.scalar.copy(v_t[:, ub, :], mm_ps[:])
+
+                y = attn.tile([P, CB, T], BF16, name="y")
+                for n in range(CB):
+                    head = slice(n * P, (n + 1) * P)
+
+                    e = attn.tile([P, TB, T], BF16, name="e")
+                    for ub in range(TB):
+                        sc_ps = psum_sc.tile([P, T], F32, name="sc_ps")
+                        nc.tensor.matmul(
+                            sc_ps[:], k[:, n, ub * P : (ub + 1) * P], q[:, n, :], start=True, stop=True
+                        )
+                        nc.scalar.activation(e[:, ub, :], sc_ps[:], FUNC.Exp, scale=SCORE_SCALE)
+
+                    sum_ps = psum_y.tile([P, T], F32, name="sum_ps")
+                    for ub in range(TB):
+                        nc.tensor.matmul(
+                            sum_ps[:], ones[:], e[:, ub, :], start=ub == 0, stop=ub == TB - 1
+                        )
+                    recip = attn.tile([P, T], F32, name="recip")
+                    nc.vector.reciprocal(recip[:], sum_ps[:])
+
+                    y_ps = psum_y.tile([P, T], F32, name="y_ps")
+                    for ub in range(TB):
+                        nc.tensor.matmul(
+                            y_ps[:], v_t[:, ub, head], e[:, ub, :], start=ub == 0, stop=ub == TB - 1
+                        )
+                    nc.vector.tensor_tensor(y[:, n, :], y_ps[:], recip[:], ALU.mult)
+
+                for ob in range(CB):
+                    mm_ps = psum_mm.tile([P, T], F32, name="mm_ps")
+                    for n in range(CB):
+                        nc.tensor.matmul(
+                            mm_ps[:],
+                            wp_sb[:, n, ob * P : (ob + 1) * P],
+                            y[:, n, :],
+                            start=n == 0,
+                            stop=n == CB - 1,
+                        )
+                    res = attn.tile([P, T], F32, name="res")
+                    nc.vector.tensor_tensor(res[:], mm_ps[:], x[ob][:, cols], ALU.add)
+                    nc.sync.dma_start(out[ob * P : (ob + 1) * P, cols], res[:])

@@ -1,4 +1,5 @@
 import concourse.mybir as mybir
+from concourse.masks import make_identity
 
 F32 = mybir.dt.float32
 BF16 = mybir.dt.bfloat16
@@ -24,11 +25,16 @@ def tile_transformernet_b_kernel(tc, emb, pos, ln_w, ln_b, wq, wk, wv, wp, offs,
     nc = tc.nc
     with (
         tc.tile_pool(name="held", bufs=1) as held,
-        tc.psum_pool(name="psum_mm", bufs=2) as psum_mm,
+        tc.tile_pool(name="qkv", bufs=B) as qkv,
+        tc.psum_pool(name="psum", bufs=1) as psum,
     ):
         offsets = held.tile([P, N // 16], U16, name="offsets")
         nc.sync.dma_start(offsets[:], offs)
 
+        wq_sb = held.tile([P, CB, C], BF16, name="wq_sb")
+        wk_sb = held.tile([P, CB, C], BF16, name="wk_sb")
+        wv_sb = held.tile([P, CB, C], BF16, name="wv_sb")
+        wp_sb = held.tile([P, CB, C], BF16, name="wp_sb")
         gain = held.tile([P, CB], F32, name="gain")
         shift = held.tile([P, CB], F32, name="shift")
         with nc.allow_non_contiguous_dma(reason="one value to a partition, 4 to a row"):
@@ -39,21 +45,19 @@ def tile_transformernet_b_kernel(tc, emb, pos, ln_w, ln_b, wq, wk, wv, wp, offs,
         nc.vector.memset(mean_w[:], 1.0 / C)
         ones = held.tile([P, P], BF16, name="ones")
         nc.vector.memset(ones[:], 1.0)
+        ident = held.tile([P, P], BF16, name="ident")
+        make_identity(nc, ident[:])
         eps = held.tile([P, 1], F32, name="eps")
         nc.vector.memset(eps[:], EPS)
 
-        wq_sb = held.tile([P, CB, C], BF16, name="wq_sb")
-        wk_sb = held.tile([P, CB, C], BF16, name="wk_sb")
-        wv_sb = held.tile([P, CB, C], BF16, name="wv_sb")
-        wp_sb = held.tile([P, CB, C], BF16, name="wp_sb")
-
         x = [held.tile([P, N], F32, name="x%d" % cb) for cb in range(CB)]
-        h = [held.tile([P, CB, T], BF16, name="h%d" % b) for b in range(B)]
+        q = []
+        k = []
+        v_t = []
 
         with (
             tc.tile_pool(name="lookup", bufs=1) as lookup,
             tc.tile_pool(name="norm", bufs=2) as norm,
-            tc.psum_pool(name="psum_stat", bufs=2) as psum_stat,
         ):
             table = []
             place = []
@@ -66,7 +70,7 @@ def tile_transformernet_b_kernel(tc, emb, pos, ln_w, ln_b, wq, wk, wv, wp, offs,
             for w_sb, w in ((wq_sb, wq), (wk_sb, wk), (wv_sb, wv), (wp_sb, wp)):
                 nc.sync.dma_start(w_sb[:], w.rearrange("(a p) o -> p a o", p=P))
 
-            for b in range(B):
+            def look_up_and_norm(b):
                 cols = slice(b * T, (b + 1) * T)
                 piece = offsets[:, b * T // 16 : (b + 1) * T // 16]
 
@@ -76,16 +80,15 @@ def tile_transformernet_b_kernel(tc, emb, pos, ln_w, ln_b, wq, wk, wv, wp, offs,
                     )
 
                 x_bf = norm.tile([P, CB, T], BF16, name="x_bf")
-                mean_ps = psum_stat.tile([P, T], F32, name="mean_ps", tag="stat")
+                mean_ps = psum.tile([P, T], F32, name="mean_ps", tag="a")
                 for cb in range(CB):
-                    nc.gpsimd.tensor_scalar(x_bf[:, cb, :], x[cb][:, cols], 1.0, None, ALU.mult)
+                    nc.vector.tensor_copy(x_bf[:, cb, :], x[cb][:, cols])
                     nc.tensor.matmul(
                         mean_ps[:], mean_w[:], x_bf[:, cb, :], start=cb == 0, stop=cb == CB - 1
                     )
-
                 centred = norm.tile([P, CB, T], F32, name="centred")
                 squared = norm.tile([P, CB, T], BF16, name="squared")
-                var_ps = psum_stat.tile([P, T], F32, name="var_ps", tag="stat")
+                var_ps = psum.tile([P, T], F32, name="var_ps", tag="b")
                 for cb in range(CB):
                     nc.vector.tensor_tensor(centred[:, cb, :], x[cb][:, cols], mean_ps[:], ALU.subtract)
                     nc.scalar.activation(squared[:, cb, :], centred[:, cb, :], FUNC.Square)
@@ -94,92 +97,125 @@ def tile_transformernet_b_kernel(tc, emb, pos, ln_w, ln_b, wq, wk, wv, wp, offs,
                     )
                 rstd = norm.tile([P, T], F32, name="rstd")
                 nc.scalar.activation(rstd[:], var_ps[:], FUNC.Abs_reciprocal_sqrt, bias=eps[:])
-
+                h = norm.tile([P, CB, T], BF16, name="h")
                 for cb in range(CB):
-                    nc.gpsimd.tensor_tensor(centred[:, cb, :], centred[:, cb, :], rstd[:], ALU.mult)
-                    nc.gpsimd.tensor_scalar(
-                        h[b][:, cb, :],
+                    nc.vector.tensor_tensor(centred[:, cb, :], centred[:, cb, :], rstd[:], ALU.mult)
+                    nc.scalar.activation(
+                        h[:, cb, :],
                         centred[:, cb, :],
-                        gain[:, cb : cb + 1],
-                        shift[:, cb : cb + 1],
-                        ALU.mult,
-                        ALU.add,
+                        FUNC.Identity,
+                        bias=shift[:, cb : cb + 1],
+                        scale=gain[:, cb : cb + 1],
                     )
+                return h
 
-        with (
-            tc.tile_pool(name="qkv", bufs=2) as qkv,
-            tc.tile_pool(name="attn", bufs=2) as attn,
-            tc.psum_pool(name="psum_y", bufs=1) as psum_y,
-            tc.psum_pool(name="psum_sc", bufs=4) as psum_sc,
-        ):
-            for b in range(B):
-                cols = slice(b * T, (b + 1) * T)
-
-                q = qkv.tile([P, CB, T], BF16, name="q")
-                k = qkv.tile([P, CB, T], BF16, name="k")
-                for w_sb, dest in ((wq_sb, q), (wk_sb, k)):
-                    for ob in range(CB):
-                        mm_ps = psum_mm.tile([P, T], F32, name="mm_ps")
+            def project(b, h):
+                q.append(qkv.tile([P, CB, T], BF16, name="q"))
+                k.append(qkv.tile([P, CB, T], BF16, name="k"))
+                v_t.append(qkv.tile([P, TB, C], BF16, name="v_t"))
+                for i in range(CB):
+                    q_ps = psum.tile([P, T], F32, name="q_ps", tag="acc", bufs=2)
+                    k_ps = psum.tile([P, T], F32, name="k_ps", tag="sc", bufs=3)
+                    for w_sb, w_ps, dest in ((wq_sb, q_ps, q[b]), (wk_sb, k_ps, k[b])):
                         for cb in range(CB):
                             nc.tensor.matmul(
-                                mm_ps[:],
-                                w_sb[:, cb, ob * P : (ob + 1) * P],
-                                h[b][:, cb, :],
+                                w_ps[:],
+                                w_sb[:, cb, i * P : (i + 1) * P],
+                                h[:, cb, :],
                                 start=cb == 0,
                                 stop=cb == CB - 1,
                             )
-                        nc.scalar.copy(dest[:, ob, :], mm_ps[:])
-
-                v_t = qkv.tile([P, TB, C], BF16, name="v_t")
-                for ub in range(TB):
-                    mm_ps = psum_mm.tile([P, T], F32, name="mm_ps")
+                        nc.scalar.copy(dest[:, i, :], w_ps[:])
+                    v_ps = psum.tile([P, T], F32, name="v_ps", tag="sc", bufs=3)
                     for cb in range(CB):
                         nc.tensor.matmul(
-                            mm_ps[:],
-                            h[b][:, cb, ub * P : (ub + 1) * P],
+                            v_ps[:],
+                            h[:, cb, i * P : (i + 1) * P],
                             wv_sb[:, cb, :],
                             start=cb == 0,
                             stop=cb == CB - 1,
                         )
-                    nc.scalar.copy(v_t[:, ub, :], mm_ps[:])
+                    nc.vector.tensor_copy(v_t[b][:, i, :], v_ps[:])
 
-                y = attn.tile([P, CB, T], BF16, name="y")
-                for n in range(CB):
-                    head = slice(n * P, (n + 1) * P)
+            h_next = look_up_and_norm(0)
+            for b in range(B):
+                h = h_next
+                if b + 1 < B:
+                    h_next = look_up_and_norm(b + 1)
+                project(b, h)
 
-                    e = attn.tile([P, TB, T], BF16, name="e")
-                    for ub in range(TB):
-                        sc_ps = psum_sc.tile([P, T], F32, name="sc_ps")
+        with tc.tile_pool(name="attn", bufs=2) as attn:
+            sums_ps = psum.tile([P, B * CB, TB], F32, name="sums_ps")
+
+            def exp_scores(b, n):
+                e = attn.tile([P, TB, T], BF16, name="e", bufs=3)
+                for ub in range(TB):
+                    sc_ps = psum.tile([P, T], F32, name="sc_ps", tag="sc", bufs=3)
+                    nc.tensor.matmul(
+                        sc_ps[:], k[b][:, n, ub * P : (ub + 1) * P], q[b][:, n, :], start=True, stop=True
+                    )
+                    nc.scalar.activation(e[:, ub, :], sc_ps[:], FUNC.Exp, scale=SCORE_SCALE)
+                return e
+
+            def weighted_values(b, n, e, y):
+                y_ps = psum.tile([P, T], F32, name="y_ps", tag="a")
+                for ub in range(TB):
+                    nc.tensor.matmul(
+                        y_ps[:],
+                        v_t[b][:, ub, n * P : (n + 1) * P],
+                        e[:, ub, :],
+                        start=ub == 0,
+                        stop=ub == TB - 1,
+                    )
+                y_raw = attn.tile([P, T], F32, name="y_raw")
+                nc.vector.tensor_copy(y_raw[:], y_ps[:])
+
+                e_pair = attn.tile([P, 2, T], BF16, name="e_pair")
+                for half in range(2):
+                    nc.gpsimd.tensor_tensor(
+                        e_pair[:, half, :], e[:, 2 * half, :], e[:, 2 * half + 1, :], ALU.add
+                    )
+                for tb in range(TB):
+                    for half in range(2):
                         nc.tensor.matmul(
-                            sc_ps[:], k[:, n, ub * P : (ub + 1) * P], q[:, n, :], start=True, stop=True
+                            sums_ps[:, CB * b + n, tb : tb + 1],
+                            e_pair[:, half, tb * P : (tb + 1) * P],
+                            ones[:, 0:1],
+                            start=half == 0,
+                            stop=half == 1,
                         )
-                        nc.scalar.activation(e[:, ub, :], sc_ps[:], FUNC.Exp, scale=SCORE_SCALE)
+                recip = attn.tile([P, TB], F32, name="recip")
+                nc.vector.reciprocal(recip[:], sums_ps[:, CB * b + n, :])
 
-                    sum_ps = psum_y.tile([P, T], F32, name="sum_ps")
-                    for ub in range(TB):
-                        nc.tensor.matmul(
-                            sum_ps[:], ones[:], e[:, ub, :], start=ub == 0, stop=ub == TB - 1
-                        )
-                    recip = attn.tile([P, T], F32, name="recip")
-                    nc.vector.reciprocal(recip[:], sum_ps[:])
+                diag = attn.tile([P, T], BF16, name="diag")
+                for tb in range(TB):
+                    nc.vector.tensor_scalar(
+                        diag[:, tb * P : (tb + 1) * P], ident[:], recip[:, tb : tb + 1], None, ALU.mult
+                    )
+                recip_ps = psum.tile([P, T], F32, name="recip_ps", tag="b")
+                nc.tensor.matmul(recip_ps[:], ones[:], diag[:], start=True, stop=True)
+                nc.vector.tensor_tensor(y[:, n, :], y_raw[:], recip_ps[:], ALU.mult)
 
-                    y_ps = psum_y.tile([P, T], F32, name="y_ps")
-                    for ub in range(TB):
-                        nc.tensor.matmul(
-                            y_ps[:], v_t[:, ub, head], e[:, ub, :], start=ub == 0, stop=ub == TB - 1
-                        )
-                    nc.vector.tensor_tensor(y[:, n, :], y_ps[:], recip[:], ALU.mult)
-
-                for ob in range(CB):
-                    mm_ps = psum_mm.tile([P, T], F32, name="mm_ps")
-                    for n in range(CB):
-                        nc.tensor.matmul(
-                            mm_ps[:],
-                            wp_sb[:, n, ob * P : (ob + 1) * P],
-                            y[:, n, :],
-                            start=n == 0,
-                            stop=n == CB - 1,
-                        )
-                    res = attn.tile([P, T], F32, name="res")
-                    nc.vector.tensor_tensor(res[:], mm_ps[:], x[ob][:, cols], ALU.add)
-                    nc.sync.dma_start(out[ob * P : (ob + 1) * P, cols], res[:])
+            heads = [(b, n) for b in range(B) for n in range(CB)]
+            e_next = exp_scores(0, 0)
+            for i, (b, n) in enumerate(heads):
+                e = e_next
+                if i + 1 < len(heads):
+                    e_next = exp_scores(heads[i + 1][0], heads[i + 1][1])
+                if n == 0:
+                    y = attn.tile([P, CB, T], BF16, name="y")
+                weighted_values(b, n, e, y)
+                if n == CB - 1:
+                    for ob in range(CB):
+                        acc = psum.tile([P, T], F32, name="acc", tag="acc", bufs=2)
+                        for cb in range(CB):
+                            nc.tensor.matmul(
+                                acc[:],
+                                wp_sb[:, cb, ob * P : (ob + 1) * P],
+                                y[:, cb, :],
+                                start=cb == 0,
+                                stop=cb == CB - 1,
+                            )
+                        res = attn.tile([P, T], F32, name="res", bufs=4)
+                        nc.vector.tensor_tensor(res[:], acc[:], x[ob][:, b * T : (b + 1) * T], ALU.add)
+                        nc.sync.dma_start(out[ob * P : (ob + 1) * P, b * T : (b + 1) * T], res[:])

@@ -16,7 +16,7 @@ T = 512
 TB = T // P
 N = B * T
 EPS = 1e-6
-SCORE_SCALE = P**-0.5
+AHEAD = 2
 
 FLOPS = 2 * (4 * C * C * N + 2 * B * CB * T * T * P)
 
@@ -26,6 +26,7 @@ def tile_transformernet_b_kernel(tc, emb, pos, ln_w, ln_b, wq, wk, wv, wp, offs,
     with (
         tc.tile_pool(name="held", bufs=1) as held,
         tc.tile_pool(name="qkv", bufs=B) as qkv,
+        tc.tile_pool(name="exps", bufs=AHEAD + 1) as exps,
         tc.psum_pool(name="psum", bufs=1) as psum,
     ):
         offsets = held.tile([P, N // 16], U16, name="offsets")
@@ -49,16 +50,34 @@ def tile_transformernet_b_kernel(tc, emb, pos, ln_w, ln_b, wq, wk, wv, wp, offs,
         make_identity(nc, ident[:])
         eps = held.tile([P, 1], F32, name="eps")
         nc.vector.memset(eps[:], EPS)
+        eps_head = held.tile([P, 1], F32, name="eps_head")
+        nc.vector.memset(eps_head[:], EPS * P)
+        columns_ps = psum.tile([P, B * CB + B, TB], F32, name="columns_ps")
+        score_scale = held.tile([P, B, TB], F32, name="score_scale")
 
         x = [held.tile([P, N], F32, name="x%d" % cb) for cb in range(CB)]
         q = []
         k = []
         v_t = []
 
+        heads = [(b, n) for b in range(B) for n in range(CB)]
+        e_of = []
+
+        def exp_scores(b, n):
+            e = exps.tile([P, TB, T], BF16, name="e")
+            for ub in range(TB):
+                sc_ps = psum.tile([P, T], F32, name="sc_ps", tag="sc", bufs=3)
+                nc.tensor.matmul(
+                    sc_ps[:], k[b][:, n, ub * P : (ub + 1) * P], q[b][:, n, :], start=True, stop=True
+                )
+                nc.scalar.activation(e[:, ub, :], sc_ps[:], FUNC.Exp, scale=score_scale[:, b, ub : ub + 1])
+            e_of.append(e)
+
         with (
             tc.tile_pool(name="lookup", bufs=1) as lookup,
             tc.tile_pool(name="norm", bufs=2) as norm,
         ):
+            nc.sync.dma_start(wk_sb[:], wk.rearrange("(a p) o -> p a o", p=P))
             table = []
             place = []
             for cb in range(CB):
@@ -67,24 +86,59 @@ def tile_transformernet_b_kernel(tc, emb, pos, ln_w, ln_b, wq, wk, wv, wp, offs,
                 nc.sync.dma_start(place[cb][:], pos[rows, 0:T])
                 table.append(lookup.tile([P, S], F32, name="table%d" % cb))
                 nc.sync.dma_start(table[cb][:], emb[rows, :])
-            for w_sb, w in ((wq_sb, wq), (wk_sb, wk), (wv_sb, wv), (wp_sb, wp)):
+            for w_sb, w in ((wq_sb, wq), (wv_sb, wv), (wp_sb, wp)):
                 nc.sync.dma_start(w_sb[:], w.rearrange("(a p) o -> p a o", p=P))
 
-            def look_up_and_norm(b):
-                cols = slice(b * T, (b + 1) * T)
-                piece = offsets[:, b * T // 16 : (b + 1) * T // 16]
+            gain_mean = lookup.tile([P, CB, P], BF16, name="gain_mean")
+            for cb in range(CB):
+                nc.vector.tensor_scalar(gain_mean[:, cb, :], mean_w[:], gain[:, cb : cb + 1], None, ALU.mult)
+            column_mean_ps = psum.tile([P, C], F32, name="column_mean_ps", tag="a")
+            for cb in range(CB):
+                nc.tensor.matmul(
+                    column_mean_ps[:], gain_mean[:, cb, :], wk_sb[:, cb, :], start=cb == 0, stop=cb == CB - 1
+                )
+            wk_c = lookup.tile([P, CB, C], BF16, name="wk_c")
+            for cb in range(CB):
+                nc.vector.scalar_tensor_tensor(
+                    wk_c[:, cb, :], wk_sb[:, cb, :], gain[:, cb : cb + 1], column_mean_ps[:], ALU.mult, ALU.subtract
+                )
 
-                for cb in range(CB):
+            x_bf = [lookup.tile([P, CB, T], BF16, name="x_bf%d" % b) for b in range(B)]
+            for cb in range(CB):
+                for b in range(B):
+                    cols = slice(b * T, (b + 1) * T)
+                    piece = offsets[:, b * T // 16 : (b + 1) * T // 16]
                     nc.vector.tensor_tensor(
                         x[cb][:, cols], table[cb][:].indirect(piece), place[cb][:], ALU.add
                     )
+                    nc.scalar.copy(x_bf[b][:, cb, :], x[cb][:, cols])
 
-                x_bf = norm.tile([P, CB, T], BF16, name="x_bf")
+            def keys(b):
+                k.append(qkv.tile([P, CB, T], BF16, name="k"))
+                for i in range(CB):
+                    if i % 2 == 0:
+                        k_ps = psum.tile([P, T], F32, name="k_ps", tag="sc", bufs=3)
+                    else:
+                        k_ps = psum.tile([P, T], F32, name="k_ps", tag="acc", bufs=2)
+                    for cb in range(CB):
+                        nc.tensor.matmul(
+                            k_ps[:],
+                            wk_c[:, cb, i * P : (i + 1) * P],
+                            x_bf[b][:, cb, :],
+                            start=cb == 0,
+                            stop=cb == CB - 1,
+                        )
+                    if i % 2 == 0:
+                        nc.scalar.copy(k[b][:, i, :], k_ps[:])
+                    else:
+                        nc.vector.tensor_copy(k[b][:, i, :], k_ps[:])
+
+            def layer_norm(b):
+                cols = slice(b * T, (b + 1) * T)
                 mean_ps = psum.tile([P, T], F32, name="mean_ps", tag="a")
                 for cb in range(CB):
-                    nc.vector.tensor_copy(x_bf[:, cb, :], x[cb][:, cols])
                     nc.tensor.matmul(
-                        mean_ps[:], mean_w[:], x_bf[:, cb, :], start=cb == 0, stop=cb == CB - 1
+                        mean_ps[:], mean_w[:], x_bf[b][:, cb, :], start=cb == 0, stop=cb == CB - 1
                     )
                 centred = norm.tile([P, CB, T], F32, name="centred")
                 squared = norm.tile([P, CB, T], BF16, name="squared")
@@ -97,6 +151,22 @@ def tile_transformernet_b_kernel(tc, emb, pos, ln_w, ln_b, wq, wk, wv, wp, offs,
                     )
                 rstd = norm.tile([P, T], F32, name="rstd")
                 nc.scalar.activation(rstd[:], var_ps[:], FUNC.Abs_reciprocal_sqrt, bias=eps[:])
+                for ub in range(TB):
+                    for cb in range(CB):
+                        nc.tensor.matmul(
+                            columns_ps[:, B * CB + b, ub : ub + 1],
+                            squared[:, cb, ub * P : (ub + 1) * P],
+                            mean_w[:, 0:1],
+                            start=cb == 0,
+                            stop=cb == CB - 1,
+                        )
+                nc.scalar.activation(
+                    score_scale[:, b, :],
+                    columns_ps[:, B * CB + b, :],
+                    FUNC.Abs_reciprocal_sqrt,
+                    bias=eps_head[:],
+                    scale=float(P),
+                )
                 h = norm.tile([P, CB, T], BF16, name="h")
                 for cb in range(CB):
                     nc.vector.tensor_tensor(centred[:, cb, :], centred[:, cb, :], rstd[:], ALU.mult)
@@ -111,21 +181,18 @@ def tile_transformernet_b_kernel(tc, emb, pos, ln_w, ln_b, wq, wk, wv, wp, offs,
 
             def project(b, h):
                 q.append(qkv.tile([P, CB, T], BF16, name="q"))
-                k.append(qkv.tile([P, CB, T], BF16, name="k"))
                 v_t.append(qkv.tile([P, TB, C], BF16, name="v_t"))
                 for i in range(CB):
                     q_ps = psum.tile([P, T], F32, name="q_ps", tag="acc", bufs=2)
-                    k_ps = psum.tile([P, T], F32, name="k_ps", tag="sc", bufs=3)
-                    for w_sb, w_ps, dest in ((wq_sb, q_ps, q[b]), (wk_sb, k_ps, k[b])):
-                        for cb in range(CB):
-                            nc.tensor.matmul(
-                                w_ps[:],
-                                w_sb[:, cb, i * P : (i + 1) * P],
-                                h[:, cb, :],
-                                start=cb == 0,
-                                stop=cb == CB - 1,
-                            )
-                        nc.scalar.copy(dest[:, i, :], w_ps[:])
+                    for cb in range(CB):
+                        nc.tensor.matmul(
+                            q_ps[:],
+                            wq_sb[:, cb, i * P : (i + 1) * P],
+                            h[:, cb, :],
+                            start=cb == 0,
+                            stop=cb == CB - 1,
+                        )
+                    nc.scalar.copy(q[b][:, i, :], q_ps[:])
                     v_ps = psum.tile([P, T], F32, name="v_ps", tag="sc", bufs=3)
                     for cb in range(CB):
                         nc.tensor.matmul(
@@ -137,26 +204,20 @@ def tile_transformernet_b_kernel(tc, emb, pos, ln_w, ln_b, wq, wk, wv, wp, offs,
                         )
                     nc.vector.tensor_copy(v_t[b][:, i, :], v_ps[:])
 
-            h_next = look_up_and_norm(0)
+            h = [layer_norm(0)]
+            keys(0)
+            h.append(layer_norm(1))
+            for b in range(1, B):
+                keys(b)
             for b in range(B):
-                h = h_next
-                if b + 1 < B:
-                    h_next = look_up_and_norm(b + 1)
-                project(b, h)
+                if b == B - 1:
+                    for b0, n0 in heads[:AHEAD]:
+                        exp_scores(b0, n0)
+                project(b, h[b])
+                if b + 2 < B:
+                    h.append(layer_norm(b + 2))
 
         with tc.tile_pool(name="attn", bufs=2) as attn:
-            sums_ps = psum.tile([P, B * CB, TB], F32, name="sums_ps")
-
-            def exp_scores(b, n):
-                e = attn.tile([P, TB, T], BF16, name="e", bufs=3)
-                for ub in range(TB):
-                    sc_ps = psum.tile([P, T], F32, name="sc_ps", tag="sc", bufs=3)
-                    nc.tensor.matmul(
-                        sc_ps[:], k[b][:, n, ub * P : (ub + 1) * P], q[b][:, n, :], start=True, stop=True
-                    )
-                    nc.scalar.activation(e[:, ub, :], sc_ps[:], FUNC.Exp, scale=SCORE_SCALE)
-                return e
-
             def weighted_values(b, n, e, y):
                 y_ps = psum.tile([P, T], F32, name="y_ps", tag="a")
                 for ub in range(TB):
@@ -178,14 +239,14 @@ def tile_transformernet_b_kernel(tc, emb, pos, ln_w, ln_b, wq, wk, wv, wp, offs,
                 for tb in range(TB):
                     for half in range(2):
                         nc.tensor.matmul(
-                            sums_ps[:, CB * b + n, tb : tb + 1],
+                            columns_ps[:, CB * b + n, tb : tb + 1],
                             e_pair[:, half, tb * P : (tb + 1) * P],
                             ones[:, 0:1],
                             start=half == 0,
                             stop=half == 1,
                         )
                 recip = attn.tile([P, TB], F32, name="recip")
-                nc.vector.reciprocal(recip[:], sums_ps[:, CB * b + n, :])
+                nc.vector.reciprocal(recip[:], columns_ps[:, CB * b + n, :])
 
                 diag = attn.tile([P, T], BF16, name="diag")
                 for tb in range(TB):
@@ -196,15 +257,12 @@ def tile_transformernet_b_kernel(tc, emb, pos, ln_w, ln_b, wq, wk, wv, wp, offs,
                 nc.tensor.matmul(recip_ps[:], ones[:], diag[:], start=True, stop=True)
                 nc.vector.tensor_tensor(y[:, n, :], y_raw[:], recip_ps[:], ALU.mult)
 
-            heads = [(b, n) for b in range(B) for n in range(CB)]
-            e_next = exp_scores(0, 0)
             for i, (b, n) in enumerate(heads):
-                e = e_next
-                if i + 1 < len(heads):
-                    e_next = exp_scores(heads[i + 1][0], heads[i + 1][1])
+                if i + AHEAD < len(heads):
+                    exp_scores(heads[i + AHEAD][0], heads[i + AHEAD][1])
                 if n == 0:
                     y = attn.tile([P, CB, T], BF16, name="y")
-                weighted_values(b, n, e, y)
+                weighted_values(b, n, e_of[i], y)
                 if n == CB - 1:
                     for ob in range(CB):
                         acc = psum.tile([P, T], F32, name="acc", tag="acc", bufs=2)

@@ -6,6 +6,7 @@ BF16 = mybir.dt.bfloat16
 U16 = mybir.dt.uint16
 ALU = mybir.AluOpType
 FUNC = mybir.ActivationFunctionType
+AXIS = mybir.AxisListType
 
 P = 128
 C = 512
@@ -52,7 +53,7 @@ def tile_transformernet_b_kernel(tc, emb, pos, ln_w, ln_b, wq, wk, wv, wp, offs,
         nc.vector.memset(eps[:], EPS)
         eps_head = held.tile([P, 1], F32, name="eps_head")
         nc.vector.memset(eps_head[:], EPS * P)
-        columns_ps = psum.tile([P, B * CB + B, TB], F32, name="columns_ps")
+        columns_ps = psum.tile([P, B * CB + B * 2 * TB, CB], F32, name="columns_ps")
         score_scale = held.tile([P, B, TB], F32, name="score_scale")
 
         x = [held.tile([P, N], F32, name="x%d" % cb) for cb in range(CB)]
@@ -112,6 +113,17 @@ def tile_transformernet_b_kernel(tc, emb, pos, ln_w, ln_b, wq, wk, wv, wp, offs,
                         x[cb][:, cols], table[cb][:].indirect(piece), place[cb][:], ALU.add
                     )
                     nc.scalar.copy(x_bf[b][:, cb, :], x[cb][:, cols])
+                    x_sq = norm.tile([P, T], BF16, name="x_sq", bufs=4)
+                    nc.scalar.activation(x_sq[:], x[cb][:, cols], FUNC.Square)
+                    for moment, summed in enumerate((x_bf[b][:, cb, :], x_sq[:])):
+                        for tb in range(TB):
+                            nc.tensor.matmul(
+                                columns_ps[:, B * CB + (2 * b + moment) * TB + tb, cb : cb + 1],
+                                summed[:, tb * P : (tb + 1) * P],
+                                mean_w[:, 0:1],
+                                start=True,
+                                stop=True,
+                            )
 
             def keys(b):
                 k.append(qkv.tile([P, CB, T], BF16, name="k"))
@@ -135,41 +147,44 @@ def tile_transformernet_b_kernel(tc, emb, pos, ln_w, ln_b, wq, wk, wv, wp, offs,
 
             def layer_norm(b):
                 cols = slice(b * T, (b + 1) * T)
-                mean_ps = psum.tile([P, T], F32, name="mean_ps", tag="a")
-                for cb in range(CB):
-                    nc.tensor.matmul(
-                        mean_ps[:], mean_w[:], x_bf[b][:, cb, :], start=cb == 0, stop=cb == CB - 1
-                    )
+                first = B * CB + 2 * b * TB
+                mean_rstd = norm.tile([P, 2, TB], F32, name="mean_rstd")
+                nc.vector.tensor_reduce(mean_rstd[:, 0, :], columns_ps[:, first : first + TB, :], AXIS.X, ALU.add)
+                var = norm.tile([P, TB], F32, name="var")
+                nc.vector.tensor_reduce(var[:], columns_ps[:, first + TB : first + 2 * TB, :], AXIS.X, ALU.add)
+                mean_sq = norm.tile([P, TB], F32, name="mean_sq")
+                nc.vector.tensor_tensor(mean_sq[:], mean_rstd[:, 0, :], mean_rstd[:, 0, :], ALU.mult)
+                nc.vector.tensor_tensor(var[:], var[:], mean_sq[:], ALU.subtract)
+                nc.scalar.activation(mean_rstd[:, 1, :], var[:], FUNC.Abs_reciprocal_sqrt, bias=eps[:])
+                nc.scalar.activation(
+                    score_scale[:, b, :], var[:], FUNC.Abs_reciprocal_sqrt, bias=eps_head[:], scale=float(P)
+                )
+                rounded = norm.tile([P, 2, TB], BF16, name="rounded")
+                nc.vector.tensor_copy(rounded[:], mean_rstd[:])
+                rest = norm.tile([P, 2, TB], F32, name="rest")
+                nc.vector.tensor_tensor(rest[:], mean_rstd[:], rounded[:], ALU.subtract)
+                spread = []
+                for which, tag in enumerate(("a", "b")):
+                    diag2 = norm.tile([P, 2, T], BF16, name="diag2")
+                    for part, values in enumerate((rounded, rest)):
+                        for tb in range(TB):
+                            nc.vector.tensor_scalar(
+                                diag2[:, part, tb * P : (tb + 1) * P],
+                                ident[:],
+                                values[:, which, tb : tb + 1],
+                                None,
+                                ALU.mult,
+                            )
+                    spread.append(psum.tile([P, T], F32, name="spread_ps", tag=tag))
+                    for part in range(2):
+                        nc.tensor.matmul(spread[which][:], ones[:], diag2[:, part, :], start=part == 0, stop=part == 1)
+                mean_ps, rstd_ps = spread
                 centred = norm.tile([P, CB, T], F32, name="centred")
-                squared = norm.tile([P, CB, T], BF16, name="squared")
-                var_ps = psum.tile([P, T], F32, name="var_ps", tag="b")
                 for cb in range(CB):
                     nc.vector.tensor_tensor(centred[:, cb, :], x[cb][:, cols], mean_ps[:], ALU.subtract)
-                    nc.scalar.activation(squared[:, cb, :], centred[:, cb, :], FUNC.Square)
-                    nc.tensor.matmul(
-                        var_ps[:], mean_w[:], squared[:, cb, :], start=cb == 0, stop=cb == CB - 1
-                    )
-                rstd = norm.tile([P, T], F32, name="rstd")
-                nc.scalar.activation(rstd[:], var_ps[:], FUNC.Abs_reciprocal_sqrt, bias=eps[:])
-                for ub in range(TB):
-                    for cb in range(CB):
-                        nc.tensor.matmul(
-                            columns_ps[:, B * CB + b, ub : ub + 1],
-                            squared[:, cb, ub * P : (ub + 1) * P],
-                            mean_w[:, 0:1],
-                            start=cb == 0,
-                            stop=cb == CB - 1,
-                        )
-                nc.scalar.activation(
-                    score_scale[:, b, :],
-                    columns_ps[:, B * CB + b, :],
-                    FUNC.Abs_reciprocal_sqrt,
-                    bias=eps_head[:],
-                    scale=float(P),
-                )
                 h = norm.tile([P, CB, T], BF16, name="h")
                 for cb in range(CB):
-                    nc.vector.tensor_tensor(centred[:, cb, :], centred[:, cb, :], rstd[:], ALU.mult)
+                    nc.vector.tensor_tensor(centred[:, cb, :], centred[:, cb, :], rstd_ps[:], ALU.mult)
                     nc.scalar.activation(
                         h[:, cb, :],
                         centred[:, cb, :],
@@ -265,7 +280,10 @@ def tile_transformernet_b_kernel(tc, emb, pos, ln_w, ln_b, wq, wk, wv, wp, offs,
                 weighted_values(b, n, e_of[i], y)
                 if n == CB - 1:
                     for ob in range(CB):
-                        acc = psum.tile([P, T], F32, name="acc", tag="acc", bufs=2)
+                        if b == B - 1 and ob >= 2:
+                            acc = psum.tile([P, T], F32, name="acc", tag="sc", bufs=3)
+                        else:
+                            acc = psum.tile([P, T], F32, name="acc", tag="acc", bufs=2)
                         for cb in range(CB):
                             nc.tensor.matmul(
                                 acc[:],

@@ -220,10 +220,9 @@ def tile_transformernet_b_kernel(tc, emb, pos, ln_w, ln_b, wq, wk, wv, wp, offs,
                     nc.vector.tensor_copy(v_t[b][:, i, :], v_ps[:])
 
             h = [layer_norm(0)]
-            keys(0)
-            h.append(layer_norm(1))
-            for b in range(1, B):
+            for b in range(B):
                 keys(b)
+            h.append(layer_norm(1))
             for b in range(B):
                 if b == B - 1:
                     for b0, n0 in heads[:AHEAD]:
@@ -248,18 +247,19 @@ def tile_transformernet_b_kernel(tc, emb, pos, ln_w, ln_b, wq, wk, wv, wp, offs,
 
                 e_pair = attn.tile([P, 2, T], BF16, name="e_pair")
                 for half in range(2):
-                    nc.gpsimd.tensor_tensor(
+                    nc.vector.tensor_tensor(
                         e_pair[:, half, :], e[:, 2 * half, :], e[:, 2 * half + 1, :], ALU.add
                     )
+                e_sum = attn.tile([P, T], BF16, name="e_sum")
+                nc.vector.tensor_tensor(e_sum[:], e_pair[:, 0, :], e_pair[:, 1, :], ALU.add)
                 for tb in range(TB):
-                    for half in range(2):
-                        nc.tensor.matmul(
-                            columns_ps[:, CB * b + n, tb : tb + 1],
-                            e_pair[:, half, tb * P : (tb + 1) * P],
-                            ones[:, 0:1],
-                            start=half == 0,
-                            stop=half == 1,
-                        )
+                    nc.tensor.matmul(
+                        columns_ps[:, CB * b + n, tb : tb + 1],
+                        e_sum[:, tb * P : (tb + 1) * P],
+                        ones[:, 0:1],
+                        start=True,
+                        stop=True,
+                    )
                 recip = attn.tile([P, TB], F32, name="recip")
                 nc.vector.reciprocal(recip[:], columns_ps[:, CB * b + n, :])
 
@@ -272,26 +272,31 @@ def tile_transformernet_b_kernel(tc, emb, pos, ln_w, ln_b, wq, wk, wv, wp, offs,
                 nc.tensor.matmul(recip_ps[:], ones[:], diag[:], start=True, stop=True)
                 nc.vector.tensor_tensor(y[:, n, :], y_raw[:], recip_ps[:], ALU.mult)
 
+            def project_out(b):
+                for ob in range(CB):
+                    if b == B - 1 and ob >= 2:
+                        acc = psum.tile([P, T], F32, name="acc", tag="sc", bufs=3)
+                    else:
+                        acc = psum.tile([P, T], F32, name="acc", tag="acc", bufs=2)
+                    for cb in range(CB):
+                        nc.tensor.matmul(
+                            acc[:],
+                            wp_sb[:, cb, ob * P : (ob + 1) * P],
+                            y_of[b][:, cb, :],
+                            start=cb == 0,
+                            stop=cb == CB - 1,
+                        )
+                    res = attn.tile([P, T], F32, name="res", bufs=4)
+                    nc.vector.tensor_tensor(res[:], acc[:], x[ob][:, b * T : (b + 1) * T], ALU.add)
+                    nc.sync.dma_start(out[ob * P : (ob + 1) * P, b * T : (b + 1) * T], res[:])
+
+            y_of = []
             for i, (b, n) in enumerate(heads):
                 if i + AHEAD < len(heads):
                     exp_scores(heads[i + AHEAD][0], heads[i + AHEAD][1])
                 if n == 0:
-                    y = attn.tile([P, CB, T], BF16, name="y")
-                weighted_values(b, n, e_of[i], y)
-                if n == CB - 1:
-                    for ob in range(CB):
-                        if b == B - 1 and ob >= 2:
-                            acc = psum.tile([P, T], F32, name="acc", tag="sc", bufs=3)
-                        else:
-                            acc = psum.tile([P, T], F32, name="acc", tag="acc", bufs=2)
-                        for cb in range(CB):
-                            nc.tensor.matmul(
-                                acc[:],
-                                wp_sb[:, cb, ob * P : (ob + 1) * P],
-                                y[:, cb, :],
-                                start=cb == 0,
-                                stop=cb == CB - 1,
-                            )
-                        res = attn.tile([P, T], F32, name="res", bufs=4)
-                        nc.vector.tensor_tensor(res[:], acc[:], x[ob][:, b * T : (b + 1) * T], ALU.add)
-                        nc.sync.dma_start(out[ob * P : (ob + 1) * P, b * T : (b + 1) * T], res[:])
+                    y_of.append(attn.tile([P, CB, T], BF16, name="y"))
+                weighted_values(b, n, e_of[i], y_of[b])
+                if n == CB - 1 and b > 0:
+                    project_out(b - 1)
+            project_out(B - 1)

@@ -19,6 +19,9 @@ N = B * T
 EPS = 1e-6
 AHEAD = 2
 
+BANKS = {"sc": 3, "acc": 2, "a": 1, "b": 1}
+ALL_BANKS = ("sc", "acc", "sc", "acc", "sc", "a", "b")
+
 FLOPS = 2 * (4 * C * C * N + 2 * B * CB * T * T * P)
 
 
@@ -128,10 +131,8 @@ def tile_transformernet_b_kernel(tc, emb, pos, ln_w, ln_b, wq, wk, wv, wp, offs,
             def keys(b):
                 k.append(qkv.tile([P, CB, T], BF16, name="k"))
                 for i in range(CB):
-                    if i % 2 == 0:
-                        k_ps = psum.tile([P, T], F32, name="k_ps", tag="sc", bufs=3)
-                    else:
-                        k_ps = psum.tile([P, T], F32, name="k_ps", tag="acc", bufs=2)
+                    tag = ALL_BANKS[(CB * b + i) % len(ALL_BANKS)]
+                    k_ps = psum.tile([P, T], F32, name="k_ps", tag=tag, bufs=BANKS[tag])
                     for cb in range(CB):
                         nc.tensor.matmul(
                             k_ps[:],
@@ -159,25 +160,15 @@ def tile_transformernet_b_kernel(tc, emb, pos, ln_w, ln_b, wq, wk, wv, wp, offs,
                 nc.scalar.activation(
                     score_scale[:, b, :], var[:], FUNC.Abs_reciprocal_sqrt, bias=eps_head[:], scale=float(P)
                 )
-                rounded = norm.tile([P, 2, TB], BF16, name="rounded")
-                nc.vector.tensor_copy(rounded[:], mean_rstd[:])
-                rest = norm.tile([P, 2, TB], F32, name="rest")
-                nc.vector.tensor_tensor(rest[:], mean_rstd[:], rounded[:], ALU.subtract)
                 spread = []
                 for which, tag in enumerate(("a", "b")):
-                    diag2 = norm.tile([P, 2, T], BF16, name="diag2")
-                    for part, values in enumerate((rounded, rest)):
-                        for tb in range(TB):
-                            nc.vector.tensor_scalar(
-                                diag2[:, part, tb * P : (tb + 1) * P],
-                                ident[:],
-                                values[:, which, tb : tb + 1],
-                                None,
-                                ALU.mult,
-                            )
+                    diag_ln = norm.tile([P, T], BF16, name="diag_ln")
+                    for tb in range(TB):
+                        nc.vector.tensor_scalar(
+                            diag_ln[:, tb * P : (tb + 1) * P], ident[:], mean_rstd[:, which, tb : tb + 1], None, ALU.mult
+                        )
                     spread.append(psum.tile([P, T], F32, name="spread_ps", tag=tag))
-                    for part in range(2):
-                        nc.tensor.matmul(spread[which][:], ones[:], diag2[:, part, :], start=part == 0, stop=part == 1)
+                    nc.tensor.matmul(spread[which][:], ones[:], diag_ln[:], start=True, stop=True)
                 mean_ps, rstd_ps = spread
                 centred = norm.tile([P, CB, T], F32, name="centred")
                 for cb in range(CB):
@@ -219,9 +210,11 @@ def tile_transformernet_b_kernel(tc, emb, pos, ln_w, ln_b, wq, wk, wv, wp, offs,
                         )
                     nc.vector.tensor_copy(v_t[b][:, i, :], v_ps[:])
 
+            keys(0)
+            keys(1)
             h = [layer_norm(0)]
-            for b in range(B):
-                keys(b)
+            keys(2)
+            keys(3)
             h.append(layer_norm(1))
             for b in range(B):
                 if b == B - 1:
@@ -243,7 +236,7 @@ def tile_transformernet_b_kernel(tc, emb, pos, ln_w, ln_b, wq, wk, wv, wp, offs,
                         stop=ub == TB - 1,
                     )
                 y_raw = attn.tile([P, T], F32, name="y_raw")
-                nc.vector.tensor_copy(y_raw[:], y_ps[:])
+                nc.scalar.copy(y_raw[:], y_ps[:])
 
                 e_pair = attn.tile([P, 2, T], BF16, name="e_pair")
                 for half in range(2):
@@ -274,7 +267,7 @@ def tile_transformernet_b_kernel(tc, emb, pos, ln_w, ln_b, wq, wk, wv, wp, offs,
 
             def project_out(b):
                 for ob in range(CB):
-                    if b == B - 1 and ob >= 2:
+                    if b >= B - 2 and ob >= 2:
                         acc = psum.tile([P, T], F32, name="acc", tag="sc", bufs=3)
                     else:
                         acc = psum.tile([P, T], F32, name="acc", tag="acc", bufs=2)

@@ -56,6 +56,8 @@ def tile_transformernet_b_kernel(tc, emb, pos, ln_w, ln_b, wq, wk, wv, wp, offs,
         nc.vector.memset(eps[:], EPS)
         eps_head = held.tile([P, 1], F32, name="eps_head")
         nc.vector.memset(eps_head[:], EPS * P)
+        unread = held.tile([P, 1], F32, name="unread")
+        nc.scalar.activation(unread[:], eps[:], FUNC.Abs_reciprocal_sqrt)
         columns_ps = psum.tile([P, B * CB + B * 2 * TB, CB], F32, name="columns_ps")
         score_scale = held.tile([P, B, TB], F32, name="score_scale")
 
@@ -149,32 +151,31 @@ def tile_transformernet_b_kernel(tc, emb, pos, ln_w, ln_b, wq, wk, wv, wp, offs,
             def layer_norm(b):
                 cols = slice(b * T, (b + 1) * T)
                 first = B * CB + 2 * b * TB
-                mean_rstd = norm.tile([P, 2, TB], F32, name="mean_rstd")
-                nc.vector.tensor_reduce(mean_rstd[:, 0, :], columns_ps[:, first : first + TB, :], AXIS.X, ALU.add)
+                moments = norm.tile([P, 2 * TB], F32, name="moments")
+                nc.vector.tensor_reduce(moments[:], columns_ps[:, first : first + 2 * TB, :], AXIS.X, ALU.add)
+                mean = moments[:, 0:TB]
                 var = norm.tile([P, TB], F32, name="var")
-                nc.vector.tensor_reduce(var[:], columns_ps[:, first + TB : first + 2 * TB, :], AXIS.X, ALU.add)
-                mean_sq = norm.tile([P, TB], F32, name="mean_sq")
-                nc.vector.tensor_tensor(mean_sq[:], mean_rstd[:, 0, :], mean_rstd[:, 0, :], ALU.mult)
-                nc.vector.tensor_tensor(var[:], var[:], mean_sq[:], ALU.subtract)
-                nc.scalar.activation(mean_rstd[:, 1, :], var[:], FUNC.Abs_reciprocal_sqrt, bias=eps[:])
+                nc.vector.tensor_tensor(var[:], mean, mean, ALU.mult)
+                nc.vector.tensor_tensor(var[:], moments[:, TB : 2 * TB], var[:], ALU.subtract)
+                rstd = norm.tile([P, TB], F32, name="rstd")
+                nc.scalar.activation(rstd[:], var[:], FUNC.Abs_reciprocal_sqrt, bias=eps[:])
                 nc.scalar.activation(
                     score_scale[:, b, :], var[:], FUNC.Abs_reciprocal_sqrt, bias=eps_head[:], scale=float(P)
                 )
                 spread = []
-                for which, tag in enumerate(("a", "b")):
+                for column, tag in ((mean, "a"), (rstd[:], "b")):
                     diag_ln = norm.tile([P, T], BF16, name="diag_ln")
                     for tb in range(TB):
                         nc.vector.tensor_scalar(
-                            diag_ln[:, tb * P : (tb + 1) * P], ident[:], mean_rstd[:, which, tb : tb + 1], None, ALU.mult
+                            diag_ln[:, tb * P : (tb + 1) * P], ident[:], column[:, tb : tb + 1], None, ALU.mult
                         )
                     spread.append(psum.tile([P, T], F32, name="spread_ps", tag=tag))
-                    nc.tensor.matmul(spread[which][:], ones[:], diag_ln[:], start=True, stop=True)
+                    nc.tensor.matmul(spread[-1][:], ones[:], diag_ln[:], start=True, stop=True)
                 mean_ps, rstd_ps = spread
                 centred = norm.tile([P, CB, T], F32, name="centred")
-                for cb in range(CB):
-                    nc.vector.tensor_tensor(centred[:, cb, :], x[cb][:, cols], mean_ps[:], ALU.subtract)
                 h = norm.tile([P, CB, T], BF16, name="h")
                 for cb in range(CB):
+                    nc.vector.tensor_tensor(centred[:, cb, :], x[cb][:, cols], mean_ps[:], ALU.subtract)
                     nc.vector.tensor_tensor(centred[:, cb, :], centred[:, cb, :], rstd_ps[:], ALU.mult)
                     nc.scalar.activation(
                         h[:, cb, :],

@@ -18,6 +18,7 @@ TB = T // P
 N = B * T
 EPS = 1e-6
 AHEAD = 2
+VW = P + 8
 
 BANKS = {"sc": 3, "acc": 2, "a": 1, "b": 1}
 ALL_BANKS = ("sc", "acc", "sc", "acc", "sc", "a", "b")
@@ -58,7 +59,6 @@ def tile_transformernet_b_kernel(tc, emb, pos, ln_w, ln_b, wq, wk, wv, wp, offs,
         nc.vector.memset(eps_head[:], EPS * P)
         unread = held.tile([P, 1], F32, name="unread")
         nc.scalar.activation(unread[:], eps[:], FUNC.Abs_reciprocal_sqrt)
-        columns_ps = psum.tile([P, B * CB + B * 2 * TB, CB], F32, name="columns_ps")
         score_scale = held.tile([P, B, TB], F32, name="score_scale")
 
         x = [held.tile([P, N], F32, name="x%d" % cb) for cb in range(CB)]
@@ -82,7 +82,9 @@ def tile_transformernet_b_kernel(tc, emb, pos, ln_w, ln_b, wq, wk, wv, wp, offs,
         with (
             tc.tile_pool(name="lookup", bufs=1) as lookup,
             tc.tile_pool(name="norm", bufs=2) as norm,
+            tc.psum_pool(name="moments_psum", bufs=1) as moments_psum,
         ):
+            columns_ps = moments_psum.tile([P, B * 2 * TB, CB], F32, name="columns_ps")
             nc.sync.dma_start(wk_sb[:], wk.rearrange("(a p) o -> p a o", p=P))
             table = []
             place = []
@@ -123,7 +125,7 @@ def tile_transformernet_b_kernel(tc, emb, pos, ln_w, ln_b, wq, wk, wv, wp, offs,
                     for moment, summed in enumerate((x_bf[b][:, cb, :], x_sq[:])):
                         for tb in range(TB):
                             nc.tensor.matmul(
-                                columns_ps[:, B * CB + (2 * b + moment) * TB + tb, cb : cb + 1],
+                                columns_ps[:, (2 * b + moment) * TB + tb, cb : cb + 1],
                                 summed[:, tb * P : (tb + 1) * P],
                                 mean_w[:, 0:1],
                                 start=True,
@@ -150,7 +152,7 @@ def tile_transformernet_b_kernel(tc, emb, pos, ln_w, ln_b, wq, wk, wv, wp, offs,
 
             def layer_norm(b):
                 cols = slice(b * T, (b + 1) * T)
-                first = B * CB + 2 * b * TB
+                first = 2 * b * TB
                 moments = norm.tile([P, 2 * TB], F32, name="moments")
                 nc.vector.tensor_reduce(moments[:], columns_ps[:, first : first + 2 * TB, :], AXIS.X, ALU.add)
                 mean = moments[:, 0:TB]
@@ -188,7 +190,8 @@ def tile_transformernet_b_kernel(tc, emb, pos, ln_w, ln_b, wq, wk, wv, wp, offs,
 
             def project(b, h):
                 q.append(qkv.tile([P, CB, T], BF16, name="q"))
-                v_t.append(qkv.tile([P, TB, C], BF16, name="v_t"))
+                v_t.append(qkv.tile([P, TB, CB, VW], BF16, name="v_t"))
+                nc.vector.memset(v_t[b][:, :, :, P : P + 1], 1.0)
                 for i in range(CB):
                     q_ps = psum.tile([P, T], F32, name="q_ps", tag="acc", bufs=2)
                     for cb in range(CB):
@@ -209,7 +212,7 @@ def tile_transformernet_b_kernel(tc, emb, pos, ln_w, ln_b, wq, wk, wv, wp, offs,
                             start=cb == 0,
                             stop=cb == CB - 1,
                         )
-                    nc.vector.tensor_copy(v_t[b][:, i, :], v_ps[:])
+                    nc.vector.tensor_copy(v_t[b][:, i, :, 0:P], v_ps[:].rearrange("p (n d) -> p n d", n=CB))
 
             keys(0)
             keys(1)
@@ -225,46 +228,34 @@ def tile_transformernet_b_kernel(tc, emb, pos, ln_w, ln_b, wq, wk, wv, wp, offs,
                 if b + 2 < B:
                     h.append(layer_norm(b + 2))
 
-        with tc.tile_pool(name="attn", bufs=2) as attn:
-            def weighted_values(b, n, e, y):
-                y_ps = psum.tile([P, T], F32, name="y_ps", tag="a")
-                for ub in range(TB):
-                    nc.tensor.matmul(
-                        y_ps[:],
-                        v_t[b][:, ub, n * P : (n + 1) * P],
-                        e[:, ub, :],
-                        start=ub == 0,
-                        stop=ub == TB - 1,
-                    )
-                y_raw = attn.tile([P, T], F32, name="y_raw")
-                nc.scalar.copy(y_raw[:], y_ps[:])
-
-                e_pair = attn.tile([P, 2, T], BF16, name="e_pair")
-                for half in range(2):
+        with tc.tile_pool(name="attn", bufs=2) as attn, tc.psum_pool(name="flip_psum", bufs=1) as flip_psum:
+            def weighted_values(b, n, e):
+                recip = attn.tile([P, TB, 1], F32, name="recip")
+                y_t = attn.tile([P, TB, P], BF16, name="y_t")
+                for half, tag in enumerate(("a", "b")):
+                    y_t_ps = psum.tile([P, 2, T // 2], F32, name="y_t_ps", tag=tag)
+                    for j in range(2):
+                        tb = 2 * half + j
+                        for ub in range(TB):
+                            nc.tensor.matmul(
+                                y_t_ps[:, j, 0 : P + 1],
+                                e[:, ub, tb * P : (tb + 1) * P],
+                                v_t[b][:, ub, n, 0 : P + 1],
+                                start=ub == 0,
+                                stop=ub == TB - 1,
+                            )
+                    both = slice(2 * half, 2 * half + 2)
+                    nc.vector.reciprocal(recip[:, both, :], y_t_ps[:, :, P : P + 1])
                     nc.vector.tensor_tensor(
-                        e_pair[:, half, :], e[:, 2 * half, :], e[:, 2 * half + 1, :], ALU.add
+                        y_t[:, both, :], y_t_ps[:, :, 0:P], recip[:, both, :].to_broadcast([P, 2, P]), ALU.mult
                     )
-                e_sum = attn.tile([P, T], BF16, name="e_sum")
-                nc.vector.tensor_tensor(e_sum[:], e_pair[:, 0, :], e_pair[:, 1, :], ALU.add)
-                for tb in range(TB):
-                    nc.tensor.matmul(
-                        columns_ps[:, CB * b + n, tb : tb + 1],
-                        e_sum[:, tb * P : (tb + 1) * P],
-                        ones[:, 0:1],
-                        start=True,
-                        stop=True,
-                    )
-                recip = attn.tile([P, TB], F32, name="recip")
-                nc.vector.reciprocal(recip[:], columns_ps[:, CB * b + n, :])
+                return y_t
 
-                diag = attn.tile([P, T], BF16, name="diag")
+            def channels_first(n, y_t, y):
+                y_ps = flip_psum.tile([P, T], BF16, name="y_ps")
                 for tb in range(TB):
-                    nc.vector.tensor_scalar(
-                        diag[:, tb * P : (tb + 1) * P], ident[:], recip[:, tb : tb + 1], None, ALU.mult
-                    )
-                recip_ps = psum.tile([P, T], F32, name="recip_ps", tag="b")
-                nc.tensor.matmul(recip_ps[:], ones[:], diag[:], start=True, stop=True)
-                nc.vector.tensor_tensor(y[:, n, :], y_raw[:], recip_ps[:], ALU.mult)
+                    nc.tensor.transpose(y_ps[:, tb * P : (tb + 1) * P], y_t[:, tb, :], ident[:])
+                nc.vector.tensor_copy(y[:, n, :], y_ps[:])
 
             def project_out(b):
                 for ob in range(CB):
@@ -285,12 +276,16 @@ def tile_transformernet_b_kernel(tc, emb, pos, ln_w, ln_b, wq, wk, wv, wp, offs,
                     nc.sync.dma_start(out[ob * P : (ob + 1) * P, b * T : (b + 1) * T], res[:])
 
             y_of = []
+            y_t_of = []
             for i, (b, n) in enumerate(heads):
                 if i + AHEAD < len(heads):
                     exp_scores(heads[i + AHEAD][0], heads[i + AHEAD][1])
                 if n == 0:
                     y_of.append(attn.tile([P, CB, T], BF16, name="y"))
-                weighted_values(b, n, e_of[i], y_of[b])
+                y_t_of.append(weighted_values(b, n, e_of[i]))
+                if i > 0:
+                    channels_first(heads[i - 1][1], y_t_of[i - 1], y_of[heads[i - 1][0]])
                 if n == CB - 1 and b > 0:
                     project_out(b - 1)
+            channels_first(CB - 1, y_t_of[-1], y_of[B - 1])
             project_out(B - 1)

@@ -166,13 +166,15 @@ def tile_transformernet_b_kernel(tc, emb, pos, ln_w, ln_b, wq, wk, wv, wp, offs,
                 )
                 spread = []
                 for column, tag in ((mean, "a"), (rstd[:], "b")):
-                    diag_ln = norm.tile([P, T], BF16, name="diag_ln")
+                    repeated = norm.tile([P, T], BF16, name="repeated")
                     for tb in range(TB):
                         nc.vector.tensor_scalar(
-                            diag_ln[:, tb * P : (tb + 1) * P], ident[:], column[:, tb : tb + 1], None, ALU.mult
+                            repeated[:, tb * P : (tb + 1) * P], ones[:], column[:, tb : tb + 1], None, ALU.mult
                         )
-                    spread.append(psum.tile([P, T], F32, name="spread_ps", tag=tag))
-                    nc.tensor.matmul(spread[-1][:], ones[:], diag_ln[:], start=True, stop=True)
+                    spread.append(psum.tile([P, T], BF16, name="spread_ps", tag=tag))
+                    for tb in range(TB):
+                        block = slice(tb * P, (tb + 1) * P)
+                        nc.tensor.transpose(spread[-1][:, block], repeated[:, block], ident[:])
                 mean_ps, rstd_ps = spread
                 centred = norm.tile([P, CB, T], F32, name="centred")
                 h = norm.tile([P, CB, T], BF16, name="h")

@@ -69,15 +69,16 @@ def tile_transformernet_b_kernel(tc, emb, pos, ln_w, ln_b, wq, wk, wv, wp, offs,
         heads = [(b, n) for b in range(B) for n in range(CB)]
         e_of = []
 
+        def exp_scores_block(b, n, ub):
+            if ub == 0:
+                e_of.append(exps.tile([P, TB, T], BF16, name="e"))
+            sc_ps = psum.tile([P, T], F32, name="sc_ps", tag="sc", bufs=3)
+            nc.tensor.matmul(sc_ps[:], k[b][:, n, ub * P : (ub + 1) * P], q[b][:, n, :], start=True, stop=True)
+            nc.scalar.activation(e_of[-1][:, ub, :], sc_ps[:], FUNC.Exp, scale=score_scale[:, b, ub : ub + 1])
+
         def exp_scores(b, n):
-            e = exps.tile([P, TB, T], BF16, name="e")
             for ub in range(TB):
-                sc_ps = psum.tile([P, T], F32, name="sc_ps", tag="sc", bufs=3)
-                nc.tensor.matmul(
-                    sc_ps[:], k[b][:, n, ub * P : (ub + 1) * P], q[b][:, n, :], start=True, stop=True
-                )
-                nc.scalar.activation(e[:, ub, :], sc_ps[:], FUNC.Exp, scale=score_scale[:, b, ub : ub + 1])
-            e_of.append(e)
+                exp_scores_block(b, n, ub)
 
         with (
             tc.tile_pool(name="lookup", bufs=1) as lookup,
@@ -195,6 +196,10 @@ def tile_transformernet_b_kernel(tc, emb, pos, ln_w, ln_b, wq, wk, wv, wp, offs,
                 v_t.append(qkv.tile([P, TB, CB, VW], BF16, name="v_t"))
                 nc.vector.memset(v_t[b][:, :, :, P : P + 1], 1.0)
                 for i in range(CB):
+                    if b == B - 1:
+                        share = AHEAD * TB // CB
+                        for j in range(share * i, share * (i + 1)):
+                            exp_scores_block(heads[j // TB][0], heads[j // TB][1], j % TB)
                     q_ps = psum.tile([P, T], F32, name="q_ps", tag="acc", bufs=2)
                     for cb in range(CB):
                         nc.tensor.matmul(
@@ -223,9 +228,6 @@ def tile_transformernet_b_kernel(tc, emb, pos, ln_w, ln_b, wq, wk, wv, wp, offs,
             keys(3)
             h.append(layer_norm(1))
             for b in range(B):
-                if b == B - 1:
-                    for b0, n0 in heads[:AHEAD]:
-                        exp_scores(b0, n0)
                 project(b, h[b])
                 if b + 2 < B:
                     h.append(layer_norm(b + 2))
@@ -260,22 +262,26 @@ def tile_transformernet_b_kernel(tc, emb, pos, ln_w, ln_b, wq, wk, wv, wp, offs,
                 nc.vector.tensor_copy(y[:, n, :], y_ps[:])
 
             def project_out(b):
-                for ob in range(CB):
-                    if b >= B - 2 and ob >= 2:
-                        acc = psum.tile([P, T], F32, name="acc", tag="sc", bufs=3)
+                pieces = [(ob, 0, T) for ob in range(CB)]
+                if b == B - 1:
+                    pieces = pieces[:-1] + [(CB - 1, 0, T // 2), (CB - 1, T // 2, T // 2)]
+                for j, (ob, first, places) in enumerate(pieces):
+                    if b >= B - 2 and j >= 2:
+                        acc = psum.tile([P, places], F32, name="acc", tag="sc", bufs=3)
                     else:
-                        acc = psum.tile([P, T], F32, name="acc", tag="acc", bufs=2)
+                        acc = psum.tile([P, places], F32, name="acc", tag="acc", bufs=2)
                     for cb in range(CB):
                         nc.tensor.matmul(
                             acc[:],
                             wp_sb[:, cb, ob * P : (ob + 1) * P],
-                            y_of[b][:, cb, :],
+                            y_of[b][:, cb, first : first + places],
                             start=cb == 0,
                             stop=cb == CB - 1,
                         )
-                    res = attn.tile([P, T], F32, name="res", bufs=4)
-                    nc.vector.tensor_tensor(res[:], acc[:], x[ob][:, b * T : (b + 1) * T], ALU.add)
-                    nc.sync.dma_start(out[ob * P : (ob + 1) * P, b * T : (b + 1) * T], res[:])
+                    cols = slice(b * T + first, b * T + first + places)
+                    res = attn.tile([P, places], F32, name="res", bufs=4)
+                    nc.vector.tensor_tensor(res[:], acc[:], x[ob][:, cols], ALU.add)
+                    nc.sync.dma_start(out[ob * P : (ob + 1) * P, cols], res[:])
 
             y_of = []
             y_t_of = []

@@ -136,7 +136,8 @@ def tile_transformernet_b_kernel(tc, emb, pos, ln_w, ln_b, wq, wk, wv, wp, offs,
             def keys(b):
                 k.append(qkv.tile([P, CB, T], BF16, name="k"))
                 for i in range(CB):
-                    tag = ALL_BANKS[(CB * b + i) % len(ALL_BANKS)]
+                    j = CB * b + i
+                    tag = ALL_BANKS[j] if j < len(ALL_BANKS) else ALL_BANKS[(j - len(ALL_BANKS)) % 5]
                     k_ps = psum.tile([P, T], F32, name="k_ps", tag=tag, bufs=BANKS[tag])
                     for cb in range(CB):
                         nc.tensor.matmul(
@@ -146,10 +147,10 @@ def tile_transformernet_b_kernel(tc, emb, pos, ln_w, ln_b, wq, wk, wv, wp, offs,
                             start=cb == 0,
                             stop=cb == CB - 1,
                         )
-                    if i % 2 == 0:
-                        nc.scalar.copy(k[b][:, i, :], k_ps[:])
-                    else:
+                    if (CB * b + i) % 3 == 1:
                         nc.vector.tensor_copy(k[b][:, i, :], k_ps[:])
+                    else:
+                        nc.scalar.copy(k[b][:, i, :], k_ps[:])
 
             def layer_norm(b):
                 cols = slice(b * T, (b + 1) * T)

import concourse.mybir as mybir
from concourse.masks import make_identity

F32 = mybir.dt.float32
BF16 = mybir.dt.bfloat16
U16 = mybir.dt.uint16
ALU = mybir.AluOpType
FUNC = mybir.ActivationFunctionType
AXIS = mybir.AxisListType

P = 128
C = 512
CB = C // P
S = 4096
B = 4
T = 512
TB = T // P
N = B * T
EPS = 1e-6
AHEAD = 2
VW = P + 8

BANKS = {"sc": 3, "acc": 2, "a": 1, "b": 1}
ALL_BANKS = ("sc", "acc", "sc", "acc", "sc", "a", "b")

FLOPS = 2 * (4 * C * C * N + 2 * B * CB * T * T * P)


def tile_transformernet_b_kernel(tc, emb, pos, ln_w, ln_b, wq, wk, wv, wp, offs, out):
    nc = tc.nc
    with (
        tc.tile_pool(name="held", bufs=1) as held,
        tc.tile_pool(name="qkv", bufs=B) as qkv,
        tc.tile_pool(name="exps", bufs=AHEAD + 1) as exps,
        tc.psum_pool(name="psum", bufs=1) as psum,
    ):
        offsets = held.tile([P, N // 16], U16, name="offsets")
        nc.sync.dma_start(offsets[:], offs)

        wq_sb = held.tile([P, CB, C], BF16, name="wq_sb")
        wk_sb = held.tile([P, CB, C], BF16, name="wk_sb")
        wv_sb = held.tile([P, CB, C], BF16, name="wv_sb")
        wp_sb = held.tile([P, CB, C], BF16, name="wp_sb")
        gain = held.tile([P, CB], F32, name="gain")
        shift = held.tile([P, CB], F32, name="shift")
        with nc.allow_non_contiguous_dma(reason="one value to a partition, 4 to a row"):
            nc.scalar.dma_start(gain[:], ln_w.rearrange("(a p) o -> p (a o)", p=P))
            nc.scalar.dma_start(shift[:], ln_b.rearrange("(a p) o -> p (a o)", p=P))

        mean_w = held.tile([P, P], BF16, name="mean_w")
        nc.vector.memset(mean_w[:], 1.0 / C)
        ones = held.tile([P, P], BF16, name="ones")
        nc.vector.memset(ones[:], 1.0)
        ident = held.tile([P, P], BF16, name="ident")
        make_identity(nc, ident[:])
        eps = held.tile([P, 1], F32, name="eps")
        nc.vector.memset(eps[:], EPS)
        eps_head = held.tile([P, 1], F32, name="eps_head")
        nc.vector.memset(eps_head[:], EPS * P)
        unread = held.tile([P, 1], F32, name="unread")
        nc.scalar.activation(unread[:], eps[:], FUNC.Abs_reciprocal_sqrt)
        score_scale = held.tile([P, B, TB], F32, name="score_scale")

        x = [held.tile([P, N], F32, name="x%d" % cb) for cb in range(CB)]
        q = []
        k = []
        v_t = []

        heads = [(b, n) for b in range(B) for n in range(CB)]
        e_of = []

        def exp_scores_block(b, n, ub):
            if ub == 0:
                e_of.append(exps.tile([P, TB, T], BF16, name="e"))
            sc_ps = psum.tile([P, T], F32, name="sc_ps", tag="sc", bufs=3)
            nc.tensor.matmul(sc_ps[:], k[b][:, n, ub * P : (ub + 1) * P], q[b][:, n, :], start=True, stop=True)
            nc.scalar.activation(e_of[-1][:, ub, :], sc_ps[:], FUNC.Exp, scale=score_scale[:, b, ub : ub + 1])

        def exp_scores(b, n):
            for ub in range(TB):
                exp_scores_block(b, n, ub)

        with (
            tc.tile_pool(name="lookup", bufs=1) as lookup,
            tc.tile_pool(name="norm", bufs=2) as norm,
            tc.psum_pool(name="moments_psum", bufs=1) as moments_psum,
        ):
            columns_ps = moments_psum.tile([P, B * 2 * TB, CB], F32, name="columns_ps")
            nc.sync.dma_start(wk_sb[:], wk.rearrange("(a p) o -> p a o", p=P))
            table = []
            place = []
            for cb in range(CB):
                rows = slice(cb * P, (cb + 1) * P)
                place.append(lookup.tile([P, T], F32, name="place%d" % cb))
                nc.sync.dma_start(place[cb][:], pos[rows, 0:T])
                table.append(lookup.tile([P, S], F32, name="table%d" % cb))
                nc.sync.dma_start(table[cb][:], emb[rows, :])
            for w_sb, w in ((wq_sb, wq), (wv_sb, wv), (wp_sb, wp)):
                nc.sync.dma_start(w_sb[:], w.rearrange("(a p) o -> p a o", p=P))

            gain_mean = lookup.tile([P, CB, P], BF16, name="gain_mean")
            for cb in range(CB):
                nc.vector.tensor_scalar(gain_mean[:, cb, :], mean_w[:], gain[:, cb : cb + 1], None, ALU.mult)
            column_mean_ps = psum.tile([P, C], F32, name="column_mean_ps", tag="a")
            for cb in range(CB):
                nc.tensor.matmul(
                    column_mean_ps[:], gain_mean[:, cb, :], wk_sb[:, cb, :], start=cb == 0, stop=cb == CB - 1
                )
            wk_c = lookup.tile([P, CB, C], BF16, name="wk_c")
            for cb in range(CB):
                nc.vector.scalar_tensor_tensor(
                    wk_c[:, cb, :], wk_sb[:, cb, :], gain[:, cb : cb + 1], column_mean_ps[:], ALU.mult, ALU.subtract
                )

            x_bf = [lookup.tile([P, CB, T], BF16, name="x_bf%d" % b) for b in range(B)]
            for cb in range(CB):
                for b in range(B):
                    cols = slice(b * T, (b + 1) * T)
                    piece = offsets[:, b * T // 16 : (b + 1) * T // 16]
                    nc.vector.tensor_tensor(
                        x[cb][:, cols], table[cb][:].indirect(piece), place[cb][:], ALU.add
                    )
                    nc.scalar.copy(x_bf[b][:, cb, :], x[cb][:, cols])
                    x_sq = norm.tile([P, T], BF16, name="x_sq", bufs=4)
                    nc.scalar.activation(x_sq[:], x[cb][:, cols], FUNC.Square)
                    for moment, summed in enumerate((x_bf[b][:, cb, :], x_sq[:])):
                        for tb in range(TB):
                            nc.tensor.matmul(
                                columns_ps[:, (2 * b + moment) * TB + tb, cb : cb + 1],
                                summed[:, tb * P : (tb + 1) * P],
                                mean_w[:, 0:1],
                                start=True,
                                stop=True,
                            )

            def keys(b):
                k.append(qkv.tile([P, CB, T], BF16, name="k"))
                for i in range(CB):
                    j = CB * b + i
                    tag = ALL_BANKS[j] if j < len(ALL_BANKS) else ALL_BANKS[(j - len(ALL_BANKS)) % 5]
                    k_ps = psum.tile([P, T], F32, name="k_ps", tag=tag, bufs=BANKS[tag])
                    for cb in range(CB):
                        nc.tensor.matmul(
                            k_ps[:],
                            wk_c[:, cb, i * P : (i + 1) * P],
                            x_bf[b][:, cb, :],
                            start=cb == 0,
                            stop=cb == CB - 1,
                        )
                    if (CB * b + i) % 3 == 1:
                        nc.vector.tensor_copy(k[b][:, i, :], k_ps[:])
                    else:
                        nc.scalar.copy(k[b][:, i, :], k_ps[:])

            def layer_norm(b):
                cols = slice(b * T, (b + 1) * T)
                first = 2 * b * TB
                moments = norm.tile([P, 2 * TB], F32, name="moments")
                nc.vector.tensor_reduce(moments[:], columns_ps[:, first : first + 2 * TB, :], AXIS.X, ALU.add)
                mean = moments[:, 0:TB]
                var = norm.tile([P, TB], F32, name="var")
                nc.vector.tensor_tensor(var[:], mean, mean, ALU.mult)
                nc.vector.tensor_tensor(var[:], moments[:, TB : 2 * TB], var[:], ALU.subtract)
                rstd = norm.tile([P, TB], F32, name="rstd")
                nc.scalar.activation(rstd[:], var[:], FUNC.Abs_reciprocal_sqrt, bias=eps[:])
                nc.scalar.activation(
                    score_scale[:, b, :], var[:], FUNC.Abs_reciprocal_sqrt, bias=eps_head[:], scale=float(P)
                )
                spread = []
                for column, tag in ((mean, "a"), (rstd[:], "b")):
                    repeated = norm.tile([P, T], BF16, name="repeated")
                    for tb in range(TB):
                        nc.vector.tensor_scalar(
                            repeated[:, tb * P : (tb + 1) * P], ones[:], column[:, tb : tb + 1], None, ALU.mult
                        )
                    spread.append(psum.tile([P, T], BF16, name="spread_ps", tag=tag))
                    for tb in range(TB):
                        block = slice(tb * P, (tb + 1) * P)
                        nc.tensor.transpose(spread[-1][:, block], repeated[:, block], ident[:])
                mean_ps, rstd_ps = spread
                centred = norm.tile([P, CB, T], F32, name="centred")
                h = norm.tile([P, CB, T], BF16, name="h")
                for cb in range(CB):
                    nc.vector.tensor_tensor(centred[:, cb, :], x[cb][:, cols], mean_ps[:], ALU.subtract)
                    nc.vector.tensor_tensor(centred[:, cb, :], centred[:, cb, :], rstd_ps[:], ALU.mult)
                    nc.scalar.activation(
                        h[:, cb, :],
                        centred[:, cb, :],
                        FUNC.Identity,
                        bias=shift[:, cb : cb + 1],
                        scale=gain[:, cb : cb + 1],
                    )
                return h

            def project(b, h):
                q.append(qkv.tile([P, CB, T], BF16, name="q"))
                v_t.append(qkv.tile([P, TB, CB, VW], BF16, name="v_t"))
                nc.vector.memset(v_t[b][:, :, :, P : P + 1], 1.0)
                for i in range(CB):
                    if b == B - 1:
                        share = AHEAD * TB // CB
                        for j in range(share * i, share * (i + 1)):
                            exp_scores_block(heads[j // TB][0], heads[j // TB][1], j % TB)
                    q_ps = psum.tile([P, T], F32, name="q_ps", tag="acc", bufs=2)
                    for cb in range(CB):
                        nc.tensor.matmul(
                            q_ps[:],
                            wq_sb[:, cb, i * P : (i + 1) * P],
                            h[:, cb, :],
                            start=cb == 0,
                            stop=cb == CB - 1,
                        )
                    nc.scalar.copy(q[b][:, i, :], q_ps[:])
                    v_ps = psum.tile([P, T], F32, name="v_ps", tag="sc", bufs=3)
                    for cb in range(CB):
                        nc.tensor.matmul(
                            v_ps[:],
                            h[:, cb, i * P : (i + 1) * P],
                            wv_sb[:, cb, :],
                            start=cb == 0,
                            stop=cb == CB - 1,
                        )
                    nc.vector.tensor_copy(v_t[b][:, i, :, 0:P], v_ps[:].rearrange("p (n d) -> p n d", n=CB))

            keys(0)
            keys(1)
            h = [layer_norm(0)]
            keys(2)
            keys(3)
            h.append(layer_norm(1))
            for b in range(B):
                project(b, h[b])
                if b + 2 < B:
                    h.append(layer_norm(b + 2))

        with tc.tile_pool(name="attn", bufs=2) as attn, tc.psum_pool(name="flip_psum", bufs=1) as flip_psum:
            def weighted_values(b, n, e):
                recip = attn.tile([P, TB, 1], F32, name="recip")
                y_t = attn.tile([P, TB, P], BF16, name="y_t")
                for half, tag in enumerate(("a", "b")):
                    y_t_ps = psum.tile([P, 2, T // 2], F32, name="y_t_ps", tag=tag)
                    for j in range(2):
                        tb = 2 * half + j
                        for ub in range(TB):
                            nc.tensor.matmul(
                                y_t_ps[:, j, 0 : P + 1],
                                e[:, ub, tb * P : (tb + 1) * P],
                                v_t[b][:, ub, n, 0 : P + 1],
                                start=ub == 0,
                                stop=ub == TB - 1,
                            )
                    both = slice(2 * half, 2 * half + 2)
                    nc.vector.reciprocal(recip[:, both, :], y_t_ps[:, :, P : P + 1])
                    nc.vector.tensor_tensor(
                        y_t[:, both, :], y_t_ps[:, :, 0:P], recip[:, both, :].to_broadcast([P, 2, P]), ALU.mult
                    )
                return y_t

            def channels_first(n, y_t, y):
                y_ps = flip_psum.tile([P, T], BF16, name="y_ps")
                for tb in range(TB):
                    nc.tensor.transpose(y_ps[:, tb * P : (tb + 1) * P], y_t[:, tb, :], ident[:])
                nc.vector.tensor_copy(y[:, n, :], y_ps[:])

            def project_out(b):
                pieces = [(ob, 0, T) for ob in range(CB)]
                if b == B - 1:
                    pieces = pieces[:-1] + [(CB - 1, 0, T // 2), (CB - 1, T // 2, T // 2)]
                for j, (ob, first, places) in enumerate(pieces):
                    if b >= B - 2 and j >= 2:
                        acc = psum.tile([P, places], F32, name="acc", tag="sc", bufs=3)
                    else:
                        acc = psum.tile([P, places], F32, name="acc", tag="acc", bufs=2)
                    for cb in range(CB):
                        nc.tensor.matmul(
                            acc[:],
                            wp_sb[:, cb, ob * P : (ob + 1) * P],
                            y_of[b][:, cb, first : first + places],
                            start=cb == 0,
                            stop=cb == CB - 1,
                        )
                    cols = slice(b * T + first, b * T + first + places)
                    res = attn.tile([P, places], F32, name="res", bufs=4)
                    nc.vector.tensor_tensor(res[:], acc[:], x[ob][:, cols], ALU.add)
                    nc.sync.dma_start(out[ob * P : (ob + 1) * P, cols], res[:])

            y_of = []
            y_t_of = []
            for i, (b, n) in enumerate(heads):
                if i + AHEAD < len(heads):
                    exp_scores(heads[i + AHEAD][0], heads[i + AHEAD][1])
                if n == 0:
                    y_of.append(attn.tile([P, CB, T], BF16, name="y"))
                y_t_of.append(weighted_values(b, n, e_of[i]))
                if i > 0:
                    channels_first(heads[i - 1][1], y_t_of[i - 1], y_of[heads[i - 1][0]])
                if n == CB - 1 and b > 0:
                    project_out(b - 1)
            channels_first(CB - 1, y_t_of[-1], y_of[B - 1])
            project_out(B - 1)
